import numpy as np
import ml_dtypes


def mxq(x, axis, fmt="e4m3"):
    dtype, down = {"e4m3": (ml_dtypes.float8_e4m3fn, 7), "e5m2": (ml_dtypes.float8_e5m2, 14)}[fmt]
    v = np.moveaxis(np.asarray(x, np.float32).astype(ml_dtypes.bfloat16).astype(np.float64), axis, -1)
    blocks = v.reshape(v.shape[:-1] + (-1, 32))
    amax = np.abs(blocks).max(-1, keepdims=True)
    byte = np.maximum(np.where(amax > 0, np.frexp(amax)[1] - 1 + 127, 0) - down, 1)
    scale = np.exp2(byte - 127.0)
    codes = (blocks / scale).astype(np.float32).astype(dtype).astype(np.float64)
    return np.moveaxis((codes * scale).reshape(v.shape), -1, axis)


WIDE = False


def mx_kscale(k):
    if not WIDE:
        return np.ones(k)
    levels = np.array([10, -10, 5, -5, 0])
    a = np.random.permutation(np.resize(levels, k // 512 * 4)).reshape(k // 512, 4)
    idx = np.arange(k)
    return np.exp2(a[idx // 512, idx % 128 // 32])


BF16 = ml_dtypes.bfloat16


def bf(x):
    return np.asarray(x, np.float32).astype(BF16)


def f64(x):
    return np.asarray(x).astype(np.float64)


NP, NH, NF, NU, B, C, H, W, IN_DIM = 7, 3, 2, 4, 8, 512, 8, 16, 256
NL = NP - 1 - NU
S = H * W
EPS = 1e-5


def make_bn():
    return bf(np.stack([1.0 + 0.1 * np.random.standard_normal(C), 0.1 * np.random.standard_normal(C),
                        0.1 * np.random.standard_normal(C), np.random.uniform(0.5, 1.5, C)]))


def make_w(col):
    return bf(np.random.standard_normal((C, col.size)) / np.sqrt(col.size) / col)


def make_nodes(n, s):
    return bf(np.random.standard_normal((n, B, C, H, W)) * s[:, None, None])


def setup_inputs():
    s = mx_kscale(C)
    return {'p_nodes': make_nodes(NP, s), 'h_nodes': make_nodes(NH, s), 'f_nodes': make_nodes(NF, s),
            'W_decomp_full': make_w(np.concatenate([s, s])), 'bn_decomp_full': make_bn(),
            'W_comp_u': make_w(np.concatenate([np.repeat(s, NU), s])), 'bn_comp_u': make_bn(),
            'W_comp_l': make_w(np.concatenate([np.repeat(s, NL), s])), 'bn_comp_l': make_bn(),
            'W_bg_h': make_w(np.concatenate([s, s, s])), 'bn_bg_h': make_bn()}


def conv(wq, xs):
    y, c0 = 0.0, 0
    for x in xs:
        c1 = c0 + x.shape[1]
        y = y + (wq[:, c0:c1] @ x)
        c0 = c1
    return y


def bn_relu(y, bn):
    gamma, beta, mean, var = f64(bn)
    scale = gamma / np.sqrt(var + EPS)
    shift = beta - mean * scale
    return np.maximum(y * scale[:, None] + shift[:, None], 0.0)


def reference(p_nodes, h_nodes, f_nodes, W_decomp_full, bn_decomp_full, W_comp_u, bn_comp_u,
              W_comp_l, bn_comp_l, W_bg_h, bn_bg_h):
    p = f64(p_nodes).reshape(NP, B, C, S)
    upper = np.moveaxis(p[1:1 + NU], 0, 2).reshape(B, NU * C, S)
    lower = np.moveaxis(p[1 + NU:], 0, 2).reshape(B, NL * C, S)
    fq = mxq(f64(f_nodes).reshape(NF, B, C, S), 2, 'e4m3')
    hq = mxq(f64(h_nodes).reshape(NH, B, C, S), 2, 'e4m3')
    p0q = mxq(p[0], 1, 'e4m3')
    uq = mxq(upper, 1, 'e4m3')
    lq = mxq(lower, 1, 'e4m3')
    wd = mxq(f64(W_decomp_full), 1, 'e4m3')
    wu = mxq(f64(W_comp_u), 1, 'e4m3')
    wl = mxq(f64(W_comp_l), 1, 'e4m3')
    wb = mxq(f64(W_bg_h), 1, 'e4m3')
    h0 = bn_relu(conv(wb, [fq[0], hq[0], p0q]), bn_bg_h)
    h1 = bn_relu(conv(wu, [uq, hq[1]]), bn_comp_u) + bn_relu(conv(wd, [fq[1], hq[1]]), bn_decomp_full)
    h2 = bn_relu(conv(wl, [lq, hq[2]]), bn_comp_l) + bn_relu(conv(wd, [fq[1], hq[2]]), bn_decomp_full)
    return np.stack([h0, h1, h2]).reshape(NH, B, C, H, W)

@@ -1,0 +1,258 @@
+from contextlib import ExitStack
+
+import concourse.mybir as mybir
+from concourse.masks import make_identity
+
+F32 = mybir.dt.float32
+BF16 = mybir.dt.bfloat16
+U32 = mybir.dt.uint32
+U8 = mybir.dt.uint8
+FP8X4 = mybir.dt.float8_e4m3fn_x4
+ACT = mybir.ActivationFunctionType
+
+P = 128
+PACK = 4
+GROUPS = 4
+PIXELS = 128
+IMAGES = 4
+COLS = IMAGES * PIXELS
+HALVES = 2
+EPS = 1e-5
+
+VECTOR_PIXELS = 96
+
+DECOMP = 0
+COMP_U = 1
+COMP_L = 2
+BG = 3
+PIECES = ((1, 1), (4, 1), (2, 1), (1, 1, 1))
+FIRST_PASS = (0, 2, 7, 10)
+WEIGHT_PASSES = 13
+
+F0 = 0
+F1 = 1
+H0 = 2
+H1 = 3
+H2 = 4
+P0 = 5
+UPPER = 6
+LOWER = 10
+MAP_PASSES = 12
+
+FLOPS = 2 * 512 * 1024 * 512 * (3 + 5 + 2 + 3 + 2)
+
+
+def tile_gnn_pa_kernel(
+    tc,
+    p_nodes,
+    h_nodes,
+    f_nodes,
+    W_decomp_full,
+    bn_decomp_full,
+    W_comp_u,
+    bn_comp_u,
+    W_comp_l,
+    bn_comp_l,
+    W_bg_h,
+    bn_bg_h,
+    out,
+):
+    nc = tc.nc
+    weights = (W_decomp_full, W_comp_u, W_comp_l, W_bg_h)
+    norms = (bn_decomp_full, bn_comp_u, bn_comp_l, bn_bg_h)
+
+    with ExitStack() as ctx:
+        const = ctx.enter_context(tc.tile_pool(name="const", bufs=1))
+        keep = ctx.enter_context(tc.tile_pool(name="keep", bufs=1))
+        raw_pool = ctx.enter_context(tc.tile_pool(name="raw", bufs=4))
+        grouped_pool = ctx.enter_context(tc.tile_pool(name="grouped", bufs=4))
+        psum = ctx.enter_context(tc.psum_pool(name="psum", bufs=8))
+
+        w_codes = keep.tile([P, WEIGHT_PASSES, GROUPS * P], U32, align_bytes=64)
+        w_scales = keep.tile([P, WEIGHT_PASSES, GROUPS * P], U8, align_bytes=64)
+        map_codes = keep.tile([P, MAP_PASSES, HALVES * COLS], U32, align_bytes=64)
+        map_scales = keep.tile([P, MAP_PASSES, HALVES * COLS], U8, align_bytes=64)
+
+        identity = const.tile([P, P], F32)
+        make_identity(nc, identity[:])
+
+        bn_rows = const.tile([P, 4, 4, GROUPS], BF16)
+        for conv in range(4):
+            nc.scalar.dma_start(
+                out=bn_rows[:, conv], in_=norms[conv].rearrange("r (m j) -> m r j", j=GROUPS)
+            )
+        bn_f32 = const.tile([P, 4, 4, GROUPS], F32)
+        nc.vector.tensor_copy(out=bn_f32[:], in_=bn_rows[:])
+        gamma, beta, mean, var = [bn_f32[:, :, row, :] for row in range(4)]
+        var_eps = const.tile([P, 4, GROUPS], F32)
+        nc.vector.tensor_scalar_add(out=var_eps[:], in0=var, scalar1=EPS)
+        std = const.tile([P, 4, GROUPS], F32)
+        nc.scalar.activation(out=std[:], in_=var_eps[:], func=ACT.Sqrt)
+        inv_std = const.tile([P, 4, GROUPS], F32)
+        nc.vector.reciprocal(out=inv_std[:], in_=std[:])
+        scale = const.tile([P, 4, GROUPS], F32)
+        nc.vector.tensor_mul(out=scale[:], in0=gamma, in1=inv_std[:])
+        mean_scaled = const.tile([P, 4, GROUPS], F32)
+        nc.vector.tensor_mul(out=mean_scaled[:], in0=mean, in1=scale[:])
+        shift = const.tile([P, 4, GROUPS], F32)
+        nc.vector.tensor_sub(out=shift[:], in0=beta, in1=mean_scaled[:])
+
+        def prepare_weight(w_pool, conv):
+            w = weights[conv]
+            w_rows = w_pool.tile([P, GROUPS, w.shape[1]], BF16, name="w_rows%d" % conv)
+            nc.sync.dma_start(out=w_rows[:], in_=w.rearrange("(m j) k -> m j k", j=GROUPS))
+            w_words = w_rows[:].bitcast(F32)
+            w_pass = FIRST_PASS[conv]
+            first_word = 0
+            for parts in PIECES[conv]:
+                piece = w_words[:, :, first_word : first_word + 2 * P * parts].rearrange(
+                    "m j (p g u) -> m j g u p", g=parts, u=2
+                )
+                for g in range(parts):
+                    grouped = grouped_pool.tile([P, GROUPS * P * PACK], BF16, tag="grouped", align_bytes=64)
+                    grouped_words = grouped[:].bitcast(F32).rearrange("p (j m u) -> p j m u", j=GROUPS, u=2)
+                    for j0, copy in ((0, nc.scalar.copy), (2, nc.vector.tensor_copy)):
+                        flipped = psum.tile([P, 2, 2, P], F32, tag="bank")
+                        for a in range(2):
+                            for u in range(2):
+                                nc.tensor.transpose(flipped[:, a, u, :], piece[:, j0 + a, g, u, :], identity[:])
+                        copy(
+                            out=grouped_words[:, j0 : j0 + 2],
+                            in_=flipped[:].rearrange("p a u m -> p a m u"),
+                        )
+                    nc.vector.quantize_mx(
+                        out=w_codes[:, w_pass, :].bitcast(FP8X4),
+                        scales=w_scales[:, w_pass, :],
+                        in_=grouped[:],
+                    )
+                    w_pass += 1
+                first_word += 2 * P * parts
+
+        with tc.tile_pool(name="w_rows", bufs=1) as w_pool:
+            for conv in range(4):
+                prepare_weight(w_pool, conv)
+
+        def load_half(nodes, half):
+            raw = raw_pool.tile([P, 4, IMAGES, PACK, PIXELS], BF16, tag="raw")
+            for slot, node in enumerate(nodes):
+                nc.sync.dma_start(
+                    out=raw[:, slot].rearrange("p b c s -> p b (c s)"),
+                    in_=node[half * IMAGES : (half + 1) * IMAGES].rearrange(
+                        "b (p c) h w -> p b (c h w)", c=PACK
+                    ),
+                )
+            return raw
+
+        def quantise(grouped, map_pass, half):
+            cols = slice(half * COLS, (half + 1) * COLS)
+            nc.vector.quantize_mx(
+                out=map_codes[:, map_pass, cols].bitcast(FP8X4),
+                scales=map_scales[:, map_pass, cols],
+                in_=grouped[:],
+            )
+
+        def quantise_rows(rows, map_pass, half):
+            grouped = grouped_pool.tile([P, COLS * PACK], BF16, tag="grouped", align_bytes=64)
+            words = grouped[:].rearrange("p (b s t) -> p b s t", b=IMAGES, t=PACK)
+            nc.vector.tensor_copy(
+                out=words[:, :, :VECTOR_PIXELS, :].rearrange("p b (c i) t -> p b c t i", i=4),
+                in_=rows[:, :, :, :VECTOR_PIXELS].rearrange("p b t (c i) -> p b c t i", i=4),
+            )
+            nc.scalar.copy(
+                out=words[:, :, VECTOR_PIXELS:, :],
+                in_=rows[:, :, :, VECTOR_PIXELS:].rearrange("p b t s -> p b s t"),
+            )
+            quantise(grouped, map_pass, half)
+
+        def quantise_node(raw, slot, map_pass, half):
+            quantise_rows(raw[:, slot], map_pass, half)
+
+        def quantise_upper(raw, half):
+            for g in range(4):
+                quantise_rows(raw[:, :, :, g, :].rearrange("p t b s -> p b t s"), UPPER + g, half)
+
+        def quantise_lower(raw, first_slot, half):
+            for g in range(2):
+                grouped = grouped_pool.tile([P, COLS * PACK], BF16, tag="grouped", align_bytes=64)
+                nc.vector.tensor_copy(
+                    out=grouped[:].rearrange("p (b s e n) -> p b s e n", b=IMAGES, e=2, n=2),
+                    in_=raw[:, first_slot : first_slot + 2, :, 2 * g : 2 * g + 2, :].rearrange(
+                        "p n b e s -> p b s e n"
+                    ),
+                )
+                quantise(grouped, LOWER + g, half)
+
+        def convolve(conv, map_passes, half):
+            cols = slice(half * COLS, (half + 1) * COLS)
+            banks = [psum.tile([P, COLS], F32, tag="bank", name="sums%d" % j) for j in range(GROUPS)]
+            last = len(map_passes) - 1
+            for k, map_pass in enumerate(map_passes):
+                w_pass = FIRST_PASS[conv] + k
+                for j in range(GROUPS):
+                    channels = slice(j * P, (j + 1) * P)
+                    nc.tensor.matmul_mx(
+                        out=banks[j][:],
+                        lhsT=w_codes[:, w_pass, channels].bitcast(FP8X4),
+                        lhsT_scale=w_scales[:, w_pass, channels],
+                        rhs=map_codes[:, map_pass, cols].bitcast(FP8X4),
+                        rhs_scale=map_scales[:, map_pass, cols],
+                        start=(k == 0),
+                        stop=(k == last),
+                    )
+            return banks
+
+        def norm_relu(dst, bank, conv, j):
+            nc.scalar.activation(
+                out=dst,
+                in_=bank[:].rearrange("p (b s) -> p b s", b=IMAGES),
+                func=ACT.Relu,
+                bias=shift[:, conv, j : j + 1],
+                scale=scale[:, conv, j : j + 1],
+            )
+
+        def store(result, h, half):
+            nc.sync.dma_start(
+                out=out[h, half * IMAGES : (half + 1) * IMAGES].rearrange(
+                    "b (m j) h w -> m b (j h w)", j=GROUPS
+                ),
+                in_=result[:].rearrange("p b j s -> p b (j s)"),
+            )
+
+        with tc.tile_pool(name="results", bufs=3) as result_pool:
+
+            def two_branches(h, half, conv, conv_passes, decomp_passes):
+                result = result_pool.tile([P, IMAGES, GROUPS, PIXELS], F32, tag="result")
+                banks = convolve(DECOMP, decomp_passes, half)
+                for j in range(GROUPS):
+                    norm_relu(result[:, :, j, :], banks[j], DECOMP, j)
+                banks = convolve(conv, conv_passes, half)
+                for j in range(GROUPS):
+                    branch = result_pool.tile([P, IMAGES, PIXELS], F32, tag="branch")
+                    norm_relu(branch[:], banks[j], conv, j)
+                    nc.vector.tensor_add(out=result[:, :, j, :], in0=result[:, :, j, :], in1=branch[:])
+                store(result, h, half)
+
+            for half in range(HALVES):
+                raw = load_half((f_nodes[1], h_nodes[1]), half)
+                quantise_node(raw, 0, F1, half)
+                quantise_node(raw, 1, H1, half)
+                raw = load_half((p_nodes[1], p_nodes[2], p_nodes[3], p_nodes[4]), half)
+                quantise_upper(raw, half)
+                two_branches(1, half, COMP_U, (UPPER, UPPER + 1, UPPER + 2, UPPER + 3, H1), (F1, H1))
+
+            for half in range(HALVES):
+                raw = load_half((h_nodes[2], p_nodes[5], p_nodes[6]), half)
+                quantise_node(raw, 0, H2, half)
+                quantise_lower(raw, 1, half)
+                two_branches(2, half, COMP_L, (LOWER, LOWER + 1, H2), (F1, H2))
+
+            for half in range(HALVES):
+                raw = load_half((f_nodes[0], h_nodes[0], p_nodes[0]), half)
+                quantise_node(raw, 0, F0, half)
+                quantise_node(raw, 1, H0, half)
+                quantise_node(raw, 2, P0, half)
+                result = result_pool.tile([P, IMAGES, GROUPS, PIXELS], F32, tag="result")
+                banks = convolve(BG, (F0, H0, P0), half)
+                for j in range(GROUPS):
+                    norm_relu(result[:, :, j, :], banks[j], BG, j)
+                store(result, 0, half)

@@ -64,8 +64,10 @@ def tile_gnn_pa_kernel(
     with ExitStack() as ctx:
         const = ctx.enter_context(tc.tile_pool(name="const", bufs=1))
         keep = ctx.enter_context(tc.tile_pool(name="keep", bufs=1))
-        raw_pool = ctx.enter_context(tc.tile_pool(name="raw", bufs=4))
+        w_pool = ctx.enter_context(tc.tile_pool(name="w_rows", bufs=2))
+        raw_pool = ctx.enter_context(tc.tile_pool(name="raw", bufs=3))
         grouped_pool = ctx.enter_context(tc.tile_pool(name="grouped", bufs=4))
+        result_pool = ctx.enter_context(tc.tile_pool(name="results", bufs=3))
         psum = ctx.enter_context(tc.psum_pool(name="psum", bufs=8))
 
         w_codes = keep.tile([P, WEIGHT_PASSES, GROUPS * P], U32, align_bytes=64)
@@ -78,28 +80,30 @@ def tile_gnn_pa_kernel(
 
         bn_rows = const.tile([P, 4, 4, GROUPS], BF16)
         for conv in range(4):
-            nc.scalar.dma_start(
+            nc.sync.dma_start(
                 out=bn_rows[:, conv], in_=norms[conv].rearrange("r (m j) -> m r j", j=GROUPS)
             )
-        bn_f32 = const.tile([P, 4, 4, GROUPS], F32)
-        nc.vector.tensor_copy(out=bn_f32[:], in_=bn_rows[:])
-        gamma, beta, mean, var = [bn_f32[:, :, row, :] for row in range(4)]
-        var_eps = const.tile([P, 4, GROUPS], F32)
-        nc.vector.tensor_scalar_add(out=var_eps[:], in0=var, scalar1=EPS)
-        std = const.tile([P, 4, GROUPS], F32)
-        nc.scalar.activation(out=std[:], in_=var_eps[:], func=ACT.Sqrt)
-        inv_std = const.tile([P, 4, GROUPS], F32)
-        nc.vector.reciprocal(out=inv_std[:], in_=std[:])
         scale = const.tile([P, 4, GROUPS], F32)
-        nc.vector.tensor_mul(out=scale[:], in0=gamma, in1=inv_std[:])
-        mean_scaled = const.tile([P, 4, GROUPS], F32)
-        nc.vector.tensor_mul(out=mean_scaled[:], in0=mean, in1=scale[:])
         shift = const.tile([P, 4, GROUPS], F32)
-        nc.vector.tensor_sub(out=shift[:], in0=beta, in1=mean_scaled[:])
 
-        def prepare_weight(w_pool, conv):
+        def fold_norms():
+            bn_f32 = const.tile([P, 4, 4, GROUPS], F32)
+            nc.vector.tensor_copy(out=bn_f32[:], in_=bn_rows[:])
+            gamma, beta, mean, var = [bn_f32[:, :, row, :] for row in range(4)]
+            var_eps = const.tile([P, 4, GROUPS], F32)
+            nc.vector.tensor_scalar_add(out=var_eps[:], in0=var, scalar1=EPS)
+            std = const.tile([P, 4, GROUPS], F32)
+            nc.scalar.activation(out=std[:], in_=var_eps[:], func=ACT.Sqrt)
+            inv_std = const.tile([P, 4, GROUPS], F32)
+            nc.vector.reciprocal(out=inv_std[:], in_=std[:])
+            nc.vector.tensor_mul(out=scale[:], in0=gamma, in1=inv_std[:])
+            mean_scaled = const.tile([P, 4, GROUPS], F32)
+            nc.vector.tensor_mul(out=mean_scaled[:], in0=mean, in1=scale[:])
+            nc.vector.tensor_sub(out=shift[:], in0=beta, in1=mean_scaled[:])
+
+        def prepare_weight(conv):
             w = weights[conv]
-            w_rows = w_pool.tile([P, GROUPS, w.shape[1]], BF16, name="w_rows%d" % conv)
+            w_rows = w_pool.tile([P, GROUPS, w.shape[1]], BF16, tag="w_rows")
             nc.sync.dma_start(out=w_rows[:], in_=w.rearrange("(m j) k -> m j k", j=GROUPS))
             w_words = w_rows[:].bitcast(F32)
             w_pass = FIRST_PASS[conv]
@@ -111,12 +115,12 @@ def tile_gnn_pa_kernel(
                 for g in range(parts):
                     grouped = grouped_pool.tile([P, GROUPS * P * PACK], BF16, tag="grouped", align_bytes=64)
                     grouped_words = grouped[:].bitcast(F32).rearrange("p (j m u) -> p j m u", j=GROUPS, u=2)
-                    for j0, copy in ((0, nc.scalar.copy), (2, nc.vector.tensor_copy)):
+                    for j0 in (0, 2):
                         flipped = psum.tile([P, 2, 2, P], F32, tag="bank")
                         for a in range(2):
                             for u in range(2):
                                 nc.tensor.transpose(flipped[:, a, u, :], piece[:, j0 + a, g, u, :], identity[:])
-                        copy(
+                        nc.scalar.copy(
                             out=grouped_words[:, j0 : j0 + 2],
                             in_=flipped[:].rearrange("p a u m -> p a m u"),
                         )
@@ -127,10 +131,6 @@ def tile_gnn_pa_kernel(
                     )
                     w_pass += 1
                 first_word += 2 * P * parts
-
-        with tc.tile_pool(name="w_rows", bufs=1) as w_pool:
-            for conv in range(4):
-                prepare_weight(w_pool, conv)
 
         def load_half(nodes, half):
             raw = raw_pool.tile([P, 4, IMAGES, PACK, PIXELS], BF16, tag="raw")
@@ -218,41 +218,44 @@ def tile_gnn_pa_kernel(
                 in_=result[:].rearrange("p b j s -> p b (j s)"),
             )
 
-        with tc.tile_pool(name="results", bufs=3) as result_pool:
+        def two_branches(h, half, conv, conv_passes, decomp_passes):
+            result = result_pool.tile([P, IMAGES, GROUPS, PIXELS], F32, tag="result")
+            banks = convolve(DECOMP, decomp_passes, half)
+            for j in range(GROUPS):
+                norm_relu(result[:, :, j, :], banks[j], DECOMP, j)
+            banks = convolve(conv, conv_passes, half)
+            for j in range(GROUPS):
+                branch = result_pool.tile([P, IMAGES, PIXELS], F32, tag="branch")
+                norm_relu(branch[:], banks[j], conv, j)
+                nc.vector.tensor_add(out=result[:, :, j, :], in0=result[:, :, j, :], in1=branch[:])
+            store(result, h, half)
 
-            def two_branches(h, half, conv, conv_passes, decomp_passes):
-                result = result_pool.tile([P, IMAGES, GROUPS, PIXELS], F32, tag="result")
-                banks = convolve(DECOMP, decomp_passes, half)
-                for j in range(GROUPS):
-                    norm_relu(result[:, :, j, :], banks[j], DECOMP, j)
-                banks = convolve(conv, conv_passes, half)
-                for j in range(GROUPS):
-                    branch = result_pool.tile([P, IMAGES, PIXELS], F32, tag="branch")
-                    norm_relu(branch[:], banks[j], conv, j)
-                    nc.vector.tensor_add(out=result[:, :, j, :], in0=result[:, :, j, :], in1=branch[:])
-                store(result, h, half)
+        prepare_weight(DECOMP)
+        prepare_weight(COMP_U)
+        fold_norms()
+        for half in range(HALVES):
+            raw = load_half((f_nodes[1], h_nodes[1]), half)
+            quantise_node(raw, 0, F1, half)
+            quantise_node(raw, 1, H1, half)
+            raw = load_half((p_nodes[1], p_nodes[2], p_nodes[3], p_nodes[4]), half)
+            quantise_upper(raw, half)
+            two_branches(1, half, COMP_U, (UPPER, UPPER + 1, UPPER + 2, UPPER + 3, H1), (F1, H1))
 
-            for half in range(HALVES):
-                raw = load_half((f_nodes[1], h_nodes[1]), half)
-                quantise_node(raw, 0, F1, half)
-                quantise_node(raw, 1, H1, half)
-                raw = load_half((p_nodes[1], p_nodes[2], p_nodes[3], p_nodes[4]), half)
-                quantise_upper(raw, half)
-                two_branches(1, half, COMP_U, (UPPER, UPPER + 1, UPPER + 2, UPPER + 3, H1), (F1, H1))
+        prepare_weight(COMP_L)
+        for half in range(HALVES):
+            raw = load_half((h_nodes[2], p_nodes[5], p_nodes[6]), half)
+            quantise_node(raw, 0, H2, half)
+            quantise_lower(raw, 1, half)
+            two_branches(2, half, COMP_L, (LOWER, LOWER + 1, H2), (F1, H2))
 
-            for half in range(HALVES):
-                raw = load_half((h_nodes[2], p_nodes[5], p_nodes[6]), half)
-                quantise_node(raw, 0, H2, half)
-                quantise_lower(raw, 1, half)
-                two_branches(2, half, COMP_L, (LOWER, LOWER + 1, H2), (F1, H2))
-
-            for half in range(HALVES):
-                raw = load_half((f_nodes[0], h_nodes[0], p_nodes[0]), half)
-                quantise_node(raw, 0, F0, half)
-                quantise_node(raw, 1, H0, half)
-                quantise_node(raw, 2, P0, half)
-                result = result_pool.tile([P, IMAGES, GROUPS, PIXELS], F32, tag="result")
-                banks = convolve(BG, (F0, H0, P0), half)
-                for j in range(GROUPS):
-                    norm_relu(result[:, :, j, :], banks[j], BG, j)
-                store(result, 0, half)
+        prepare_weight(BG)
+        for half in range(HALVES):
+            raw = load_half((f_nodes[0], h_nodes[0], p_nodes[0]), half)
+            quantise_node(raw, 0, F0, half)
+            quantise_node(raw, 1, H0, half)
+            quantise_node(raw, 2, P0, half)
+            result = result_pool.tile([P, IMAGES, GROUPS, PIXELS], F32, tag="result")
+            banks = convolve(BG, (F0, H0, P0), half)
+            for j in range(GROUPS):
+                norm_relu(result[:, :, j, :], banks[j], BG, j)
+            store(result, 0, half)

@@ -29,15 +29,15 @@ PIECES = ((1, 1), (4, 1), (2, 1), (1, 1, 1))
 FIRST_PASS = (0, 2, 7, 10)
 WEIGHT_PASSES = 13
 
-F0 = 0
-F1 = 1
-H0 = 2
-H1 = 3
-H2 = 4
-P0 = 5
-UPPER = 6
-LOWER = 10
-MAP_PASSES = 12
+F1 = 0
+H2 = 1
+H1 = 2
+UPPER = 3
+P0 = H1
+LOWER = UPPER
+F0 = UPPER + 2
+H0 = UPPER + 3
+MAP_PASSES = 7
 
 FLOPS = 2 * 512 * 1024 * 512 * (3 + 5 + 2 + 3 + 2)
 
@@ -64,8 +64,8 @@ def tile_gnn_pa_kernel(
     with ExitStack() as ctx:
         const = ctx.enter_context(tc.tile_pool(name="const", bufs=1))
         keep = ctx.enter_context(tc.tile_pool(name="keep", bufs=1))
-        w_pool = ctx.enter_context(tc.tile_pool(name="w_rows", bufs=2))
-        raw_pool = ctx.enter_context(tc.tile_pool(name="raw", bufs=3))
+        w_pool = ctx.enter_context(tc.tile_pool(name="w_rows", bufs=1))
+        raw_pool = ctx.enter_context(tc.tile_pool(name="raw", bufs=4))
         grouped_pool = ctx.enter_context(tc.tile_pool(name="grouped", bufs=4))
         result_pool = ctx.enter_context(tc.tile_pool(name="results", bufs=3))
         psum = ctx.enter_context(tc.psum_pool(name="psum", bufs=8))
@@ -101,10 +101,13 @@ def tile_gnn_pa_kernel(
             nc.vector.tensor_mul(out=mean_scaled[:], in0=mean, in1=scale[:])
             nc.vector.tensor_sub(out=shift[:], in0=beta, in1=mean_scaled[:])
 
-        def prepare_weight(conv):
+        def load_weight(conv):
             w = weights[conv]
-            w_rows = w_pool.tile([P, GROUPS, w.shape[1]], BF16, tag="w_rows")
+            w_rows = w_pool.tile([P, GROUPS, w.shape[1]], BF16, name="w_rows%d" % conv)
             nc.sync.dma_start(out=w_rows[:], in_=w.rearrange("(m j) k -> m j k", j=GROUPS))
+            return w_rows
+
+        def prepare_weight(conv, w_rows):
             w_words = w_rows[:].bitcast(F32)
             w_pass = FIRST_PASS[conv]
             first_word = 0
@@ -151,7 +154,7 @@ def tile_gnn_pa_kernel(
                 in_=grouped[:],
             )
 
-        def quantise_rows(rows, map_pass, half):
+        def regroup_rows(rows):
             grouped = grouped_pool.tile([P, COLS * PACK], BF16, tag="grouped", align_bytes=64)
             words = grouped[:].rearrange("p (b s t) -> p b s t", b=IMAGES, t=PACK)
             nc.vector.tensor_copy(
@@ -162,25 +165,39 @@ def tile_gnn_pa_kernel(
                 out=words[:, :, VECTOR_PIXELS:, :],
                 in_=rows[:, :, :, VECTOR_PIXELS:].rearrange("p b t s -> p b s t"),
             )
-            quantise(grouped, map_pass, half)
+            return grouped
 
-        def quantise_node(raw, slot, map_pass, half):
-            quantise_rows(raw[:, slot], map_pass, half)
+        def regroup_pairs(pairs):
+            grouped = grouped_pool.tile([P, COLS * PACK], BF16, tag="grouped", align_bytes=64)
+            nc.vector.tensor_copy(
+                out=grouped[:].rearrange("p (b s e n) -> p b s e n", b=IMAGES, e=2, n=2),
+                in_=pairs.rearrange("p n b e s -> p b s e n"),
+            )
+            return grouped
 
-        def quantise_upper(raw, half):
-            for g in range(4):
-                quantise_rows(raw[:, :, :, g, :].rearrange("p t b s -> p b t s"), UPPER + g, half)
+        def node_job(raw, slot, map_pass):
+            return (regroup_rows, raw[:, slot], map_pass)
 
-        def quantise_lower(raw, first_slot, half):
-            for g in range(2):
-                grouped = grouped_pool.tile([P, COLS * PACK], BF16, tag="grouped", align_bytes=64)
-                nc.vector.tensor_copy(
-                    out=grouped[:].rearrange("p (b s e n) -> p b s e n", b=IMAGES, e=2, n=2),
-                    in_=raw[:, first_slot : first_slot + 2, :, 2 * g : 2 * g + 2, :].rearrange(
-                        "p n b e s -> p b s e n"
-                    ),
-                )
-                quantise(grouped, LOWER + g, half)
+        def upper_jobs(raw):
+            return [
+                (regroup_rows, raw[:, :, :, g, :].rearrange("p t b s -> p b t s"), UPPER + g)
+                for g in range(4)
+            ]
+
+        def lower_jobs(raw, first_slot):
+            return [
+                (regroup_pairs, raw[:, first_slot : first_slot + 2, :, 2 * g : 2 * g + 2, :], LOWER + g)
+                for g in range(2)
+            ]
+
+        def quantise_jobs(jobs, half):
+            waiting = None
+            for regroup, view, map_pass in jobs:
+                grouped = regroup(view)
+                if waiting is not None:
+                    quantise(waiting[0], waiting[1], half)
+                waiting = (grouped, map_pass)
+            quantise(waiting[0], waiting[1], half)
 
         def convolve(conv, map_passes, half):
             cols = slice(half * COLS, (half + 1) * COLS)
@@ -230,32 +247,60 @@ def tile_gnn_pa_kernel(
                 nc.vector.tensor_add(out=result[:, :, j, :], in0=result[:, :, j, :], in1=branch[:])
             store(result, h, half)
 
-        prepare_weight(DECOMP)
-        prepare_weight(COMP_U)
-        fold_norms()
-        for half in range(HALVES):
-            raw = load_half((f_nodes[1], h_nodes[1]), half)
-            quantise_node(raw, 0, F1, half)
-            quantise_node(raw, 1, H1, half)
-            raw = load_half((p_nodes[1], p_nodes[2], p_nodes[3], p_nodes[4]), half)
-            quantise_upper(raw, half)
-            two_branches(1, half, COMP_U, (UPPER, UPPER + 1, UPPER + 2, UPPER + 3, H1), (F1, H1))
-
-        prepare_weight(COMP_L)
-        for half in range(HALVES):
-            raw = load_half((h_nodes[2], p_nodes[5], p_nodes[6]), half)
-            quantise_node(raw, 0, H2, half)
-            quantise_lower(raw, 1, half)
-            two_branches(2, half, COMP_L, (LOWER, LOWER + 1, H2), (F1, H2))
-
-        prepare_weight(BG)
-        for half in range(HALVES):
-            raw = load_half((f_nodes[0], h_nodes[0], p_nodes[0]), half)
-            quantise_node(raw, 0, F0, half)
-            quantise_node(raw, 1, H0, half)
-            quantise_node(raw, 2, P0, half)
+        def one_branch(h, half, conv, conv_passes):
             result = result_pool.tile([P, IMAGES, GROUPS, PIXELS], F32, tag="result")
-            banks = convolve(BG, (F0, H0, P0), half)
+            banks = convolve(conv, conv_passes, half)
             for j in range(GROUPS):
-                norm_relu(result[:, :, j, :], banks[j], BG, j)
-            store(result, 0, half)
+                norm_relu(result[:, :, j, :], banks[j], conv, j)
+            store(result, h, half)
+
+        rounds = [(h, half) for h in (1, 2, 0) for half in range(HALVES)]
+        first_use = {1: (DECOMP, COMP_U), 2: (COMP_L,), 0: (BG,)}
+        w_rows = {}
+        raws = {}
+
+        def load_round(h, half):
+            if half == 0:
+                for conv in first_use[h]:
+                    w_rows[conv] = load_weight(conv)
+            if h == 1:
+                raws[h, half] = (
+                    load_half((f_nodes[1], h_nodes[1]), half),
+                    load_half((p_nodes[1], p_nodes[2], p_nodes[3], p_nodes[4]), half),
+                )
+            elif h == 2:
+                raws[h, half] = load_half((h_nodes[2], p_nodes[5], p_nodes[6]), half)
+            else:
+                raws[h, half] = load_half((f_nodes[0], h_nodes[0], p_nodes[0]), half)
+
+        def quantise_round(h, half):
+            if half == 0:
+                for conv in first_use[h]:
+                    prepare_weight(conv, w_rows[conv])
+            raw = raws[h, half]
+            if h == 1:
+                jobs = [node_job(raw[0], 0, F1), node_job(raw[0], 1, H1)] + upper_jobs(raw[1])
+            elif h == 2:
+                jobs = [node_job(raw, 0, H2)] + lower_jobs(raw, 1)
+            else:
+                jobs = [node_job(raw, 0, F0), node_job(raw, 1, H0), node_job(raw, 2, P0)]
+            quantise_jobs(jobs, half)
+
+        def finish_round(h, half):
+            if h == 1:
+                two_branches(1, half, COMP_U, (UPPER, UPPER + 1, UPPER + 2, UPPER + 3, H1), (F1, H1))
+            elif h == 2:
+                two_branches(2, half, COMP_L, (LOWER, LOWER + 1, H2), (F1, H2))
+            else:
+                one_branch(0, half, BG, (F0, H0, P0))
+
+        load_round(*rounds[0])
+        load_round(*rounds[1])
+        quantise_round(*rounds[0])
+        fold_norms()
+        for r in range(len(rounds)):
+            if r + 2 < len(rounds):
+                load_round(*rounds[r + 2])
+            if r + 1 < len(rounds):
+                quantise_round(*rounds[r + 1])
+            finish_round(*rounds[r])

@@ -14,9 +14,8 @@ P = 128
 PACK = 4
 GROUPS = 4
 PIXELS = 128
-IMAGES = 4
-COLS = IMAGES * PIXELS
-HALVES = 2
+BATCH = 8
+MAX_IMAGES = 4
 EPS = 1e-5
 
 VECTOR_PIXELS = 96
@@ -39,7 +38,22 @@ F0 = UPPER + 2
 H0 = UPPER + 3
 MAP_PASSES = 7
 
+ROUNDS = (
+    (1, (0, 4)),
+    (1, (4, 4)),
+    (2, (0, 4)),
+    (2, (4, 4)),
+    (0, (0, 4)),
+    (0, (4, 2)),
+    (0, (6, 2)),
+)
+
 FLOPS = 2 * 512 * 1024 * 512 * (3 + 5 + 2 + 3 + 2)
+
+
+def columns(images):
+    first, count = images
+    return slice(first * PIXELS, (first + count) * PIXELS)
 
 
 def tile_gnn_pa_kernel(
@@ -72,8 +86,8 @@ def tile_gnn_pa_kernel(
 
         w_codes = keep.tile([P, WEIGHT_PASSES, GROUPS * P], U32, align_bytes=64)
         w_scales = keep.tile([P, WEIGHT_PASSES, GROUPS * P], U8, align_bytes=64)
-        map_codes = keep.tile([P, MAP_PASSES, HALVES * COLS], U32, align_bytes=64)
-        map_scales = keep.tile([P, MAP_PASSES, HALVES * COLS], U8, align_bytes=64)
+        map_codes = keep.tile([P, MAP_PASSES, BATCH * PIXELS], U32, align_bytes=64)
+        map_scales = keep.tile([P, MAP_PASSES, BATCH * PIXELS], U8, align_bytes=64)
 
         identity = const.tile([P, P], F32)
         make_identity(nc, identity[:])
@@ -135,28 +149,21 @@ def tile_gnn_pa_kernel(
                     w_pass += 1
                 first_word += 2 * P * parts
 
-        def load_half(nodes, half):
-            raw = raw_pool.tile([P, 4, IMAGES, PACK, PIXELS], BF16, tag="raw")
+        def load_maps(nodes, images):
+            first, count = images
+            raw = raw_pool.tile([P, 4, MAX_IMAGES, PACK, PIXELS], BF16, tag="raw")
             for slot, node in enumerate(nodes):
                 nc.sync.dma_start(
-                    out=raw[:, slot].rearrange("p b c s -> p b (c s)"),
-                    in_=node[half * IMAGES : (half + 1) * IMAGES].rearrange(
-                        "b (p c) h w -> p b (c h w)", c=PACK
-                    ),
+                    out=raw[:, slot, :count].rearrange("p b c s -> p b (c s)"),
+                    in_=node[first : first + count].rearrange("b (p c) h w -> p b (c h w)", c=PACK),
                 )
-            return raw
-
-        def quantise(grouped, map_pass, half):
-            cols = slice(half * COLS, (half + 1) * COLS)
-            nc.vector.quantize_mx(
-                out=map_codes[:, map_pass, cols].bitcast(FP8X4),
-                scales=map_scales[:, map_pass, cols],
-                in_=grouped[:],
-            )
+            return raw[:, :, :count]
 
         def regroup_rows(rows):
-            grouped = grouped_pool.tile([P, COLS * PACK], BF16, tag="grouped", align_bytes=64)
-            words = grouped[:].rearrange("p (b s t) -> p b s t", b=IMAGES, t=PACK)
+            count = rows.shape[1]
+            whole = grouped_pool.tile([P, MAX_IMAGES * PIXELS * PACK], BF16, tag="grouped", align_bytes=64)
+            grouped = whole[:, : count * PIXELS * PACK]
+            words = grouped.rearrange("p (b s t) -> p b s t", b=count, t=PACK)
             nc.vector.tensor_copy(
                 out=words[:, :, :VECTOR_PIXELS, :].rearrange("p b (c i) t -> p b c t i", i=4),
                 in_=rows[:, :, :, :VECTOR_PIXELS].rearrange("p b t (c i) -> p b c t i", i=4),
@@ -168,9 +175,11 @@ def tile_gnn_pa_kernel(
             return grouped
 
         def regroup_pairs(pairs):
-            grouped = grouped_pool.tile([P, COLS * PACK], BF16, tag="grouped", align_bytes=64)
+            count = pairs.shape[2]
+            whole = grouped_pool.tile([P, MAX_IMAGES * PIXELS * PACK], BF16, tag="grouped", align_bytes=64)
+            grouped = whole[:, : count * PIXELS * PACK]
             nc.vector.tensor_copy(
-                out=grouped[:].rearrange("p (b s e n) -> p b s e n", b=IMAGES, e=2, n=2),
+                out=grouped.rearrange("p (b s e n) -> p b s e n", b=count, e=2, n=2),
                 in_=pairs.rearrange("p n b e s -> p b s e n"),
             )
             return grouped
@@ -190,117 +199,113 @@ def tile_gnn_pa_kernel(
                 for g in range(2)
             ]
 
-        def quantise_jobs(jobs, half):
+        def quantise(grouped, map_pass, images):
+            nc.vector.quantize_mx(
+                out=map_codes[:, map_pass, columns(images)].bitcast(FP8X4),
+                scales=map_scales[:, map_pass, columns(images)],
+                in_=grouped,
+            )
+
+        def quantise_jobs(jobs, images):
             waiting = None
             for regroup, view, map_pass in jobs:
                 grouped = regroup(view)
                 if waiting is not None:
-                    quantise(waiting[0], waiting[1], half)
+                    quantise(waiting[0], waiting[1], images)
                 waiting = (grouped, map_pass)
-            quantise(waiting[0], waiting[1], half)
+            quantise(waiting[0], waiting[1], images)
 
-        def convolve(conv, map_passes, half):
-            cols = slice(half * COLS, (half + 1) * COLS)
-            banks = [psum.tile([P, COLS], F32, tag="bank", name="sums%d" % j) for j in range(GROUPS)]
+        def convolve(conv, map_passes, images):
+            width = images[1] * PIXELS
+            banks = [psum.tile([P, MAX_IMAGES * PIXELS], F32, tag="bank", name="sums%d" % j) for j in range(GROUPS)]
             last = len(map_passes) - 1
             for k, map_pass in enumerate(map_passes):
                 w_pass = FIRST_PASS[conv] + k
                 for j in range(GROUPS):
                     channels = slice(j * P, (j + 1) * P)
                     nc.tensor.matmul_mx(
-                        out=banks[j][:],
+                        out=banks[j][:, :width],
                         lhsT=w_codes[:, w_pass, channels].bitcast(FP8X4),
                         lhsT_scale=w_scales[:, w_pass, channels],
-                        rhs=map_codes[:, map_pass, cols].bitcast(FP8X4),
-                        rhs_scale=map_scales[:, map_pass, cols],
+                        rhs=map_codes[:, map_pass, columns(images)].bitcast(FP8X4),
+                        rhs_scale=map_scales[:, map_pass, columns(images)],
                         start=(k == 0),
                         stop=(k == last),
                     )
-            return banks
+            return [bank[:, :width] for bank in banks]
 
-        def norm_relu(dst, bank, conv, j):
+        def norm_relu(dst, sums, conv, j):
             nc.scalar.activation(
                 out=dst,
-                in_=bank[:].rearrange("p (b s) -> p b s", b=IMAGES),
+                in_=sums.rearrange("p (b s) -> p b s", s=PIXELS),
                 func=ACT.Relu,
                 bias=shift[:, conv, j : j + 1],
                 scale=scale[:, conv, j : j + 1],
             )
 
-        def store(result, h, half):
+        branches = {
+            1: ((DECOMP, (F1, H1)), (COMP_U, (UPPER, UPPER + 1, UPPER + 2, UPPER + 3, H1))),
+            2: ((DECOMP, (F1, H2)), (COMP_L, (LOWER, LOWER + 1, H2))),
+            0: ((BG, (F0, H0, P0)),),
+        }
+
+        def finish_round(h, images):
+            first, count = images
+            whole = result_pool.tile([P, MAX_IMAGES, GROUPS, PIXELS], F32, tag="result")
+            result = whole[:, :count]
+            conv, map_passes = branches[h][0]
+            sums = convolve(conv, map_passes, images)
+            for j in range(GROUPS):
+                norm_relu(result[:, :, j, :], sums[j], conv, j)
+            for conv, map_passes in branches[h][1:]:
+                sums = convolve(conv, map_passes, images)
+                for j in range(GROUPS):
+                    branch = result_pool.tile([P, MAX_IMAGES, PIXELS], F32, tag="branch")
+                    norm_relu(branch[:, :count], sums[j], conv, j)
+                    nc.vector.tensor_add(out=result[:, :, j, :], in0=result[:, :, j, :], in1=branch[:, :count])
             nc.sync.dma_start(
-                out=out[h, half * IMAGES : (half + 1) * IMAGES].rearrange(
-                    "b (m j) h w -> m b (j h w)", j=GROUPS
-                ),
-                in_=result[:].rearrange("p b j s -> p b (j s)"),
+                out=out[h, first : first + count].rearrange("b (m j) h w -> m b (j h w)", j=GROUPS),
+                in_=result.rearrange("p b j s -> p b (j s)"),
             )
 
-        def two_branches(h, half, conv, conv_passes, decomp_passes):
-            result = result_pool.tile([P, IMAGES, GROUPS, PIXELS], F32, tag="result")
-            banks = convolve(DECOMP, decomp_passes, half)
-            for j in range(GROUPS):
-                norm_relu(result[:, :, j, :], banks[j], DECOMP, j)
-            banks = convolve(conv, conv_passes, half)
-            for j in range(GROUPS):
-                branch = result_pool.tile([P, IMAGES, PIXELS], F32, tag="branch")
-                norm_relu(branch[:], banks[j], conv, j)
-                nc.vector.tensor_add(out=result[:, :, j, :], in0=result[:, :, j, :], in1=branch[:])
-            store(result, h, half)
-
-        def one_branch(h, half, conv, conv_passes):
-            result = result_pool.tile([P, IMAGES, GROUPS, PIXELS], F32, tag="result")
-            banks = convolve(conv, conv_passes, half)
-            for j in range(GROUPS):
-                norm_relu(result[:, :, j, :], banks[j], conv, j)
-            store(result, h, half)
-
-        rounds = [(h, half) for h in (1, 2, 0) for half in range(HALVES)]
-        first_use = {1: (DECOMP, COMP_U), 2: (COMP_L,), 0: (BG,)}
+        first_use = {1: DECOMP, 2: COMP_L, 0: BG}
         w_rows = {}
         raws = {}
 
-        def load_round(h, half):
-            if half == 0:
-                for conv in first_use[h]:
-                    w_rows[conv] = load_weight(conv)
+        def load_round(h, images):
+            if images[0] == 0:
+                w_rows[first_use[h]] = load_weight(first_use[h])
             if h == 1:
-                raws[h, half] = (
-                    load_half((f_nodes[1], h_nodes[1]), half),
-                    load_half((p_nodes[1], p_nodes[2], p_nodes[3], p_nodes[4]), half),
+                raws[h, images] = (
+                    load_maps((f_nodes[1], h_nodes[1]), images),
+                    load_maps((p_nodes[1], p_nodes[2], p_nodes[3], p_nodes[4]), images),
                 )
             elif h == 2:
-                raws[h, half] = load_half((h_nodes[2], p_nodes[5], p_nodes[6]), half)
+                raws[h, images] = load_maps((h_nodes[2], p_nodes[5], p_nodes[6]), images)
             else:
-                raws[h, half] = load_half((f_nodes[0], h_nodes[0], p_nodes[0]), half)
+                raws[h, images] = load_maps((f_nodes[0], h_nodes[0], p_nodes[0]), images)
 
-        def quantise_round(h, half):
-            if half == 0:
-                for conv in first_use[h]:
-                    prepare_weight(conv, w_rows[conv])
-            raw = raws[h, half]
+        def quantise_round(h, images):
+            if images[0] == 0:
+                prepare_weight(first_use[h], w_rows[first_use[h]])
+            raw = raws[h, images]
             if h == 1:
                 jobs = [node_job(raw[0], 0, F1), node_job(raw[0], 1, H1)] + upper_jobs(raw[1])
             elif h == 2:
                 jobs = [node_job(raw, 0, H2)] + lower_jobs(raw, 1)
             else:
                 jobs = [node_job(raw, 0, F0), node_job(raw, 1, H0), node_job(raw, 2, P0)]
-            quantise_jobs(jobs, half)
+            quantise_jobs(jobs, images)
 
-        def finish_round(h, half):
-            if h == 1:
-                two_branches(1, half, COMP_U, (UPPER, UPPER + 1, UPPER + 2, UPPER + 3, H1), (F1, H1))
-            elif h == 2:
-                two_branches(2, half, COMP_L, (LOWER, LOWER + 1, H2), (F1, H2))
-            else:
-                one_branch(0, half, BG, (F0, H0, P0))
-
-        load_round(*rounds[0])
-        load_round(*rounds[1])
-        quantise_round(*rounds[0])
+        load_round(*ROUNDS[0])
+        w_rows[COMP_U] = load_weight(COMP_U)
+        load_round(*ROUNDS[1])
+        quantise_round(*ROUNDS[0])
+        prepare_weight(COMP_U, w_rows[COMP_U])
         fold_norms()
-        for r in range(len(rounds)):
-            if r + 2 < len(rounds):
-                load_round(*rounds[r + 2])
-            if r + 1 < len(rounds):
-                quantise_round(*rounds[r + 1])
-            finish_round(*rounds[r])
+        for r in range(len(ROUNDS)):
+            if r + 2 < len(ROUNDS):
+                load_round(*ROUNDS[r + 2])
+            if r + 1 < len(ROUNDS):
+                quantise_round(*ROUNDS[r + 1])
+            finish_round(*ROUNDS[r])

@@ -27,6 +27,8 @@ BG = 3
 PIECES = ((1, 1), (4, 1), (2, 1), (1, 1, 1))
 FIRST_PASS = (0, 2, 7, 10)
 WEIGHT_PASSES = 13
+W_TAGS = ("w_decomp", "w_large", "w_comp_l", "w_large")
+NODE_TILES = 6
 
 F1 = 0
 H2 = 1
@@ -79,7 +81,8 @@ def tile_gnn_pa_kernel(
         const = ctx.enter_context(tc.tile_pool(name="const", bufs=1))
         keep = ctx.enter_context(tc.tile_pool(name="keep", bufs=1))
         w_pool = ctx.enter_context(tc.tile_pool(name="w_rows", bufs=1))
-        raw_pool = ctx.enter_context(tc.tile_pool(name="raw", bufs=4))
+        raw_pool = ctx.enter_context(tc.tile_pool(name="raw", bufs=2))
+        node_pool = ctx.enter_context(tc.tile_pool(name="nodes", bufs=NODE_TILES))
         grouped_pool = ctx.enter_context(tc.tile_pool(name="grouped", bufs=4))
         result_pool = ctx.enter_context(tc.tile_pool(name="results", bufs=3))
         psum = ctx.enter_context(tc.psum_pool(name="psum", bufs=8))
@@ -117,7 +120,7 @@ def tile_gnn_pa_kernel(
 
         def load_weight(conv):
             w = weights[conv]
-            w_rows = w_pool.tile([P, GROUPS, w.shape[1]], BF16, name="w_rows%d" % conv)
+            w_rows = w_pool.tile([P, GROUPS, w.shape[1]], BF16, name="w_rows%d" % conv, tag=W_TAGS[conv])
             nc.sync.dma_start(out=w_rows[:], in_=w.rearrange("(m j) k -> m j k", j=GROUPS))
             return w_rows
 
@@ -151,7 +154,10 @@ def tile_gnn_pa_kernel(
 
         def load_maps(nodes, images):
             first, count = images
-            raw = raw_pool.tile([P, 4, MAX_IMAGES, PACK, PIXELS], BF16, tag="raw")
+            if len(nodes) == 1:
+                raw = node_pool.tile([P, 1, MAX_IMAGES, PACK, PIXELS], BF16, tag="node")
+            else:
+                raw = raw_pool.tile([P, len(nodes), MAX_IMAGES, PACK, PIXELS], BF16, tag="raw%d" % len(nodes))
             for slot, node in enumerate(nodes):
                 nc.sync.dma_start(
                     out=raw[:, slot, :count].rearrange("p b c s -> p b (c s)"),
@@ -277,35 +283,42 @@ def tile_gnn_pa_kernel(
                 w_rows[first_use[h]] = load_weight(first_use[h])
             if h == 1:
                 raws[h, images] = (
-                    load_maps((f_nodes[1], h_nodes[1]), images),
+                    load_maps((f_nodes[1],), images),
+                    load_maps((h_nodes[1],), images),
                     load_maps((p_nodes[1], p_nodes[2], p_nodes[3], p_nodes[4]), images),
                 )
             elif h == 2:
-                raws[h, images] = load_maps((h_nodes[2], p_nodes[5], p_nodes[6]), images)
+                raws[h, images] = (
+                    load_maps((h_nodes[2],), images),
+                    load_maps((p_nodes[5], p_nodes[6]), images),
+                )
             else:
-                raws[h, images] = load_maps((f_nodes[0], h_nodes[0], p_nodes[0]), images)
+                raws[h, images] = (
+                    load_maps((f_nodes[0],), images),
+                    load_maps((h_nodes[0],), images),
+                    load_maps((p_nodes[0],), images),
+                )
 
         def quantise_round(h, images):
             if images[0] == 0:
                 prepare_weight(first_use[h], w_rows[first_use[h]])
             raw = raws[h, images]
             if h == 1:
-                jobs = [node_job(raw[0], 0, F1), node_job(raw[0], 1, H1)] + upper_jobs(raw[1])
+                jobs = [node_job(raw[0], 0, F1), node_job(raw[1], 0, H1)] + upper_jobs(raw[2])
             elif h == 2:
-                jobs = [node_job(raw, 0, H2)] + lower_jobs(raw, 1)
+                jobs = [node_job(raw[0], 0, H2)] + lower_jobs(raw[1], 0)
             else:
-                jobs = [node_job(raw, 0, F0), node_job(raw, 1, H0), node_job(raw, 2, P0)]
+                jobs = [node_job(raw[0], 0, F0), node_job(raw[1], 0, H0), node_job(raw[2], 0, P0)]
             quantise_jobs(jobs, images)
 
         load_round(*ROUNDS[0])
         w_rows[COMP_U] = load_weight(COMP_U)
-        load_round(*ROUNDS[1])
+        for r in range(1, len(ROUNDS)):
+            load_round(*ROUNDS[r])
         quantise_round(*ROUNDS[0])
         prepare_weight(COMP_U, w_rows[COMP_U])
         fold_norms()
         for r in range(len(ROUNDS)):
-            if r + 2 < len(ROUNDS):
-                load_round(*ROUNDS[r + 2])
             if r + 1 < len(ROUNDS):
                 quantise_round(*ROUNDS[r + 1])
             finish_round(*ROUNDS[r])

@@ -29,6 +29,7 @@ FIRST_PASS = (0, 2, 7, 10)
 WEIGHT_PASSES = 13
 W_TAGS = ("w_decomp", "w_large", "w_comp_l", "w_large")
 NODE_TILES = 6
+IN_TWO_LOADS = (DECOMP, COMP_U)
 
 F1 = 0
 H2 = 1
@@ -121,36 +122,52 @@ def tile_gnn_pa_kernel(
         def load_weight(conv):
             w = weights[conv]
             w_rows = w_pool.tile([P, GROUPS, w.shape[1]], BF16, name="w_rows%d" % conv, tag=W_TAGS[conv])
-            nc.sync.dma_start(out=w_rows[:], in_=w.rearrange("(m j) k -> m j k", j=GROUPS))
+            rows = w.rearrange("(m j) k -> m j k", j=GROUPS)
+            if conv in IN_TWO_LOADS:
+                for j0 in (0, 2):
+                    nc.sync.dma_start(out=w_rows[:, j0 : j0 + 2], in_=rows[:, j0 : j0 + 2])
+            else:
+                nc.sync.dma_start(out=w_rows[:], in_=rows)
             return w_rows
 
-        def prepare_weight(conv, w_rows):
+        def prepare_passes(conv, w_rows, groups):
             w_words = w_rows[:].bitcast(F32)
             w_pass = FIRST_PASS[conv]
             first_word = 0
+            channels = slice(groups[0] * P, (groups[-1] + 1) * P)
             for parts in PIECES[conv]:
                 piece = w_words[:, :, first_word : first_word + 2 * P * parts].rearrange(
                     "m j (p g u) -> m j g u p", g=parts, u=2
                 )
                 for g in range(parts):
-                    grouped = grouped_pool.tile([P, GROUPS * P * PACK], BF16, tag="grouped", align_bytes=64)
-                    grouped_words = grouped[:].bitcast(F32).rearrange("p (j m u) -> p j m u", j=GROUPS, u=2)
-                    for j0 in (0, 2):
+                    whole = grouped_pool.tile([P, GROUPS * P * PACK], BF16, tag="grouped", align_bytes=64)
+                    grouped = whole[:, : len(groups) * P * PACK]
+                    grouped_words = grouped.bitcast(F32).rearrange("p (j m u) -> p j m u", j=len(groups), u=2)
+                    for j0 in range(0, len(groups), 2):
                         flipped = psum.tile([P, 2, 2, P], F32, tag="bank")
                         for a in range(2):
                             for u in range(2):
-                                nc.tensor.transpose(flipped[:, a, u, :], piece[:, j0 + a, g, u, :], identity[:])
+                                nc.tensor.transpose(
+                                    flipped[:, a, u, :], piece[:, groups[j0 + a], g, u, :], identity[:]
+                                )
                         nc.scalar.copy(
                             out=grouped_words[:, j0 : j0 + 2],
                             in_=flipped[:].rearrange("p a u m -> p a m u"),
                         )
                     nc.vector.quantize_mx(
-                        out=w_codes[:, w_pass, :].bitcast(FP8X4),
-                        scales=w_scales[:, w_pass, :],
-                        in_=grouped[:],
+                        out=w_codes[:, w_pass, channels].bitcast(FP8X4),
+                        scales=w_scales[:, w_pass, channels],
+                        in_=grouped,
                     )
                     w_pass += 1
                 first_word += 2 * P * parts
+
+        def prepare_weight(conv, w_rows):
+            if conv in IN_TWO_LOADS:
+                prepare_passes(conv, w_rows, (0, 1))
+                prepare_passes(conv, w_rows, (2, 3))
+            else:
+                prepare_passes(conv, w_rows, (0, 1, 2, 3))
 
         def load_maps(nodes, images):
             first, count = images

from contextlib import ExitStack

import concourse.mybir as mybir
from concourse.masks import make_identity

F32 = mybir.dt.float32
BF16 = mybir.dt.bfloat16
U32 = mybir.dt.uint32
U8 = mybir.dt.uint8
FP8X4 = mybir.dt.float8_e4m3fn_x4
ACT = mybir.ActivationFunctionType

P = 128
PACK = 4
GROUPS = 4
PIXELS = 128
BATCH = 8
MAX_IMAGES = 4
EPS = 1e-5

VECTOR_PIXELS = 96

DECOMP = 0
COMP_U = 1
COMP_L = 2
BG = 3
PIECES = ((1, 1), (4, 1), (2, 1), (1, 1, 1))
FIRST_PASS = (0, 2, 7, 10)
WEIGHT_PASSES = 13
W_TAGS = ("w_decomp", "w_large", "w_comp_l", "w_large")
NODE_TILES = 6
IN_TWO_LOADS = (DECOMP, COMP_U)

F1 = 0
H2 = 1
H1 = 2
UPPER = 3
P0 = H1
LOWER = UPPER
F0 = UPPER + 2
H0 = UPPER + 3
MAP_PASSES = 7

ROUNDS = (
    (1, (0, 4)),
    (1, (4, 4)),
    (2, (0, 4)),
    (2, (4, 4)),
    (0, (0, 4)),
    (0, (4, 2)),
    (0, (6, 2)),
)

FLOPS = 2 * 512 * 1024 * 512 * (3 + 5 + 2 + 3 + 2)


def columns(images):
    first, count = images
    return slice(first * PIXELS, (first + count) * PIXELS)


def tile_gnn_pa_kernel(
    tc,
    p_nodes,
    h_nodes,
    f_nodes,
    W_decomp_full,
    bn_decomp_full,
    W_comp_u,
    bn_comp_u,
    W_comp_l,
    bn_comp_l,
    W_bg_h,
    bn_bg_h,
    out,
):
    nc = tc.nc
    weights = (W_decomp_full, W_comp_u, W_comp_l, W_bg_h)
    norms = (bn_decomp_full, bn_comp_u, bn_comp_l, bn_bg_h)

    with ExitStack() as ctx:
        const = ctx.enter_context(tc.tile_pool(name="const", bufs=1))
        keep = ctx.enter_context(tc.tile_pool(name="keep", bufs=1))
        w_pool = ctx.enter_context(tc.tile_pool(name="w_rows", bufs=1))
        raw_pool = ctx.enter_context(tc.tile_pool(name="raw", bufs=2))
        node_pool = ctx.enter_context(tc.tile_pool(name="nodes", bufs=NODE_TILES))
        grouped_pool = ctx.enter_context(tc.tile_pool(name="grouped", bufs=4))
        result_pool = ctx.enter_context(tc.tile_pool(name="results", bufs=3))
        psum = ctx.enter_context(tc.psum_pool(name="psum", bufs=8))

        w_codes = keep.tile([P, WEIGHT_PASSES, GROUPS * P], U32, align_bytes=64)
        w_scales = keep.tile([P, WEIGHT_PASSES, GROUPS * P], U8, align_bytes=64)
        map_codes = keep.tile([P, MAP_PASSES, BATCH * PIXELS], U32, align_bytes=64)
        map_scales = keep.tile([P, MAP_PASSES, BATCH * PIXELS], U8, align_bytes=64)

        identity = const.tile([P, P], F32)
        make_identity(nc, identity[:])

        bn_rows = const.tile([P, 4, 4, GROUPS], BF16)
        for conv in range(4):
            nc.sync.dma_start(
                out=bn_rows[:, conv], in_=norms[conv].rearrange("r (m j) -> m r j", j=GROUPS)
            )
        scale = const.tile([P, 4, GROUPS], F32)
        shift = const.tile([P, 4, GROUPS], F32)

        def fold_norms():
            bn_f32 = const.tile([P, 4, 4, GROUPS], F32)
            nc.vector.tensor_copy(out=bn_f32[:], in_=bn_rows[:])
            gamma, beta, mean, var = [bn_f32[:, :, row, :] for row in range(4)]
            var_eps = const.tile([P, 4, GROUPS], F32)
            nc.vector.tensor_scalar_add(out=var_eps[:], in0=var, scalar1=EPS)
            std = const.tile([P, 4, GROUPS], F32)
            nc.scalar.activation(out=std[:], in_=var_eps[:], func=ACT.Sqrt)
            inv_std = const.tile([P, 4, GROUPS], F32)
            nc.vector.reciprocal(out=inv_std[:], in_=std[:])
            nc.vector.tensor_mul(out=scale[:], in0=gamma, in1=inv_std[:])
            mean_scaled = const.tile([P, 4, GROUPS], F32)
            nc.vector.tensor_mul(out=mean_scaled[:], in0=mean, in1=scale[:])
            nc.vector.tensor_sub(out=shift[:], in0=beta, in1=mean_scaled[:])

        def load_weight(conv):
            w = weights[conv]
            w_rows = w_pool.tile([P, GROUPS, w.shape[1]], BF16, name="w_rows%d" % conv, tag=W_TAGS[conv])
            rows = w.rearrange("(m j) k -> m j k", j=GROUPS)
            if conv in IN_TWO_LOADS:
                for j0 in (0, 2):
                    nc.sync.dma_start(out=w_rows[:, j0 : j0 + 2], in_=rows[:, j0 : j0 + 2])
            else:
                nc.sync.dma_start(out=w_rows[:], in_=rows)
            return w_rows

        def prepare_passes(conv, w_rows, groups):
            w_words = w_rows[:].bitcast(F32)
            w_pass = FIRST_PASS[conv]
            first_word = 0
            channels = slice(groups[0] * P, (groups[-1] + 1) * P)
            for parts in PIECES[conv]:
                piece = w_words[:, :, first_word : first_word + 2 * P * parts].rearrange(
                    "m j (p g u) -> m j g u p", g=parts, u=2
                )
                for g in range(parts):
                    whole = grouped_pool.tile([P, GROUPS * P * PACK], BF16, tag="grouped", align_bytes=64)
                    grouped = whole[:, : len(groups) * P * PACK]
                    grouped_words = grouped.bitcast(F32).rearrange("p (j m u) -> p j m u", j=len(groups), u=2)
                    for j0 in range(0, len(groups), 2):
                        flipped = psum.tile([P, 2, 2, P], F32, tag="bank")
                        for a in range(2):
                            for u in range(2):
                                nc.tensor.transpose(
                                    flipped[:, a, u, :], piece[:, groups[j0 + a], g, u, :], identity[:]
                                )
                        nc.scalar.copy(
                            out=grouped_words[:, j0 : j0 + 2],
                            in_=flipped[:].rearrange("p a u m -> p a m u"),
                        )
                    nc.vector.quantize_mx(
                        out=w_codes[:, w_pass, channels].bitcast(FP8X4),
                        scales=w_scales[:, w_pass, channels],
                        in_=grouped,
                    )
                    w_pass += 1
                first_word += 2 * P * parts

        def prepare_weight(conv, w_rows):
            if conv in IN_TWO_LOADS:
                prepare_passes(conv, w_rows, (0, 1))
                prepare_passes(conv, w_rows, (2, 3))
            else:
                prepare_passes(conv, w_rows, (0, 1, 2, 3))

        def load_maps(nodes, images):
            first, count = images
            if len(nodes) == 1:
                raw = node_pool.tile([P, 1, MAX_IMAGES, PACK, PIXELS], BF16, tag="node")
            else:
                raw = raw_pool.tile([P, len(nodes), MAX_IMAGES, PACK, PIXELS], BF16, tag="raw%d" % len(nodes))
            for slot, node in enumerate(nodes):
                nc.sync.dma_start(
                    out=raw[:, slot, :count].rearrange("p b c s -> p b (c s)"),
                    in_=node[first : first + count].rearrange("b (p c) h w -> p b (c h w)", c=PACK),
                )
            return raw[:, :, :count]

        def regroup_rows(rows):
            count = rows.shape[1]
            whole = grouped_pool.tile([P, MAX_IMAGES * PIXELS * PACK], BF16, tag="grouped", align_bytes=64)
            grouped = whole[:, : count * PIXELS * PACK]
            words = grouped.rearrange("p (b s t) -> p b s t", b=count, t=PACK)
            nc.vector.tensor_copy(
                out=words[:, :, :VECTOR_PIXELS, :].rearrange("p b (c i) t -> p b c t i", i=4),
                in_=rows[:, :, :, :VECTOR_PIXELS].rearrange("p b t (c i) -> p b c t i", i=4),
            )
            nc.scalar.copy(
                out=words[:, :, VECTOR_PIXELS:, :],
                in_=rows[:, :, :, VECTOR_PIXELS:].rearrange("p b t s -> p b s t"),
            )
            return grouped

        def regroup_pairs(pairs):
            count = pairs.shape[2]
            whole = grouped_pool.tile([P, MAX_IMAGES * PIXELS * PACK], BF16, tag="grouped", align_bytes=64)
            grouped = whole[:, : count * PIXELS * PACK]
            nc.vector.tensor_copy(
                out=grouped.rearrange("p (b s e n) -> p b s e n", b=count, e=2, n=2),
                in_=pairs.rearrange("p n b e s -> p b s e n"),
            )
            return grouped

        def node_job(raw, slot, map_pass):
            return (regroup_rows, raw[:, slot], map_pass)

        def upper_jobs(raw):
            return [
                (regroup_rows, raw[:, :, :, g, :].rearrange("p t b s -> p b t s"), UPPER + g)
                for g in range(4)
            ]

        def lower_jobs(raw, first_slot):
            return [
                (regroup_pairs, raw[:, first_slot : first_slot + 2, :, 2 * g : 2 * g + 2, :], LOWER + g)
                for g in range(2)
            ]

        def quantise(grouped, map_pass, images):
            nc.vector.quantize_mx(
                out=map_codes[:, map_pass, columns(images)].bitcast(FP8X4),
                scales=map_scales[:, map_pass, columns(images)],
                in_=grouped,
            )

        def quantise_jobs(jobs, images):
            waiting = None
            for regroup, view, map_pass in jobs:
                grouped = regroup(view)
                if waiting is not None:
                    quantise(waiting[0], waiting[1], images)
                waiting = (grouped, map_pass)
            quantise(waiting[0], waiting[1], images)

        def convolve(conv, map_passes, images):
            width = images[1] * PIXELS
            banks = [psum.tile([P, MAX_IMAGES * PIXELS], F32, tag="bank", name="sums%d" % j) for j in range(GROUPS)]
            last = len(map_passes) - 1
            for k, map_pass in enumerate(map_passes):
                w_pass = FIRST_PASS[conv] + k
                for j in range(GROUPS):
                    channels = slice(j * P, (j + 1) * P)
                    nc.tensor.matmul_mx(
                        out=banks[j][:, :width],
                        lhsT=w_codes[:, w_pass, channels].bitcast(FP8X4),
                        lhsT_scale=w_scales[:, w_pass, channels],
                        rhs=map_codes[:, map_pass, columns(images)].bitcast(FP8X4),
                        rhs_scale=map_scales[:, map_pass, columns(images)],
                        start=(k == 0),
                        stop=(k == last),
                    )
            return [bank[:, :width] for bank in banks]

        def norm_relu(dst, sums, conv, j):
            nc.scalar.activation(
                out=dst,
                in_=sums.rearrange("p (b s) -> p b s", s=PIXELS),
                func=ACT.Relu,
                bias=shift[:, conv, j : j + 1],
                scale=scale[:, conv, j : j + 1],
            )

        branches = {
            1: ((DECOMP, (F1, H1)), (COMP_U, (UPPER, UPPER + 1, UPPER + 2, UPPER + 3, H1))),
            2: ((DECOMP, (F1, H2)), (COMP_L, (LOWER, LOWER + 1, H2))),
            0: ((BG, (F0, H0, P0)),),
        }

        def finish_round(h, images):
            first, count = images
            whole = result_pool.tile([P, MAX_IMAGES, GROUPS, PIXELS], F32, tag="result")
            result = whole[:, :count]
            conv, map_passes = branches[h][0]
            sums = convolve(conv, map_passes, images)
            for j in range(GROUPS):
                norm_relu(result[:, :, j, :], sums[j], conv, j)
            for conv, map_passes in branches[h][1:]:
                sums = convolve(conv, map_passes, images)
                for j in range(GROUPS):
                    branch = result_pool.tile([P, MAX_IMAGES, PIXELS], F32, tag="branch")
                    norm_relu(branch[:, :count], sums[j], conv, j)
                    nc.vector.tensor_add(out=result[:, :, j, :], in0=result[:, :, j, :], in1=branch[:, :count])
            nc.sync.dma_start(
                out=out[h, first : first + count].rearrange("b (m j) h w -> m b (j h w)", j=GROUPS),
                in_=result.rearrange("p b j s -> p b (j s)"),
            )

        first_use = {1: DECOMP, 2: COMP_L, 0: BG}
        w_rows = {}
        raws = {}

        def load_round(h, images):
            if images[0] == 0:
                w_rows[first_use[h]] = load_weight(first_use[h])
            if h == 1:
                raws[h, images] = (
                    load_maps((f_nodes[1],), images),
                    load_maps((h_nodes[1],), images),
                    load_maps((p_nodes[1], p_nodes[2], p_nodes[3], p_nodes[4]), images),
                )
            elif h == 2:
                raws[h, images] = (
                    load_maps((h_nodes[2],), images),
                    load_maps((p_nodes[5], p_nodes[6]), images),
                )
            else:
                raws[h, images] = (
                    load_maps((f_nodes[0],), images),
                    load_maps((h_nodes[0],), images),
                    load_maps((p_nodes[0],), images),
                )

        def quantise_round(h, images):
            if images[0] == 0:
                prepare_weight(first_use[h], w_rows[first_use[h]])
            raw = raws[h, images]
            if h == 1:
                jobs = [node_job(raw[0], 0, F1), node_job(raw[1], 0, H1)] + upper_jobs(raw[2])
            elif h == 2:
                jobs = [node_job(raw[0], 0, H2)] + lower_jobs(raw[1], 0)
            else:
                jobs = [node_job(raw[0], 0, F0), node_job(raw[1], 0, H0), node_job(raw[2], 0, P0)]
            quantise_jobs(jobs, images)

        load_round(*ROUNDS[0])
        w_rows[COMP_U] = load_weight(COMP_U)
        for r in range(1, len(ROUNDS)):
            load_round(*ROUNDS[r])
        quantise_round(*ROUNDS[0])
        prepare_weight(COMP_U, w_rows[COMP_U])
        fold_norms()
        for r in range(len(ROUNDS)):
            if r + 1 < len(ROUNDS):
                quantise_round(*ROUNDS[r + 1])
            finish_round(*ROUNDS[r])
